import numpy as np
import ml_dtypes


BF16 = ml_dtypes.bfloat16


def bf(x):
    return np.asarray(x, np.float32).astype(BF16)


def f64(x):
    return np.asarray(x).astype(np.float64)


E2M1 = np.array([0.0, 0.5, 1.0, 1.5, 2.0, 3.0, 4.0, 6.0, -0.0, -0.5, -1.0, -1.5, -2.0, -3.0, -4.0, -6.0])


def pack_weight(w, fmt):
    k, n = w.shape
    w = f64(bf(w)).reshape(k // 32, 32, n)
    amax = np.abs(w).max(1)
    if fmt == "e4m3":
        byte = np.frexp(amax)[1] - 1 + 127 - 7
    else:
        mant, ex = np.frexp(amax / 6.0)
        byte = np.where(mant > 0.5, ex, ex - 1) + 127
    byte = np.clip(np.where(amax > 0, byte, 1), 1, 254)
    scaled = (w * np.exp2(127.0 - byte)[:, None, :]).reshape(k, n).astype(np.float32)
    by_word = np.ascontiguousarray(scaled.reshape(k // 512, 128, 4, n).transpose(0, 1, 3, 2))
    if fmt == "e4m3":
        words = by_word.astype(ml_dtypes.float8_e4m3fn).view(np.uint8)
    else:
        c = by_word.astype(ml_dtypes.float4_e2m1fn).view(np.uint8) & 0xF
        words = c[..., 0::2] | (c[..., 1::2] << 4)
    return np.ascontiguousarray(words), np.ascontiguousarray(byte.astype(np.uint8).reshape(k // 512, 16, n))


def unpack_weight(words, scales, fmt):
    g, p, n, _ = words.shape
    if fmt == "e4m3":
        vals = np.ascontiguousarray(words).view(ml_dtypes.float8_e4m3fn).astype(np.float64)
    else:
        nib = np.empty((g, p, n, 4), np.uint8)
        nib[..., 0::2] = words & 0xF
        nib[..., 1::2] = words >> 4
        vals = E2M1[nib]
    vals = vals * np.repeat(np.exp2(scales.astype(np.float64) - 127.0), 8, axis=1)[..., None]
    return vals.transpose(0, 1, 3, 2).reshape(g * 512, n)

def pack4(w):
    words, scales = pack_weight(w, "e2m1")
    return words.reshape(words.shape[0], 128, -1), scales


def unpack4(words, scales):
    return unpack_weight(words.reshape(words.shape[0], 128, -1, 2), scales, "e2m1")


def kspread(k):
    return np.exp2(np.repeat(np.random.randint(-6, 7, k // 32), 32).astype(np.float64))


B, S, HID, H, D = 1, 384, 4096, 8, 128
QKV = 3 * H * D


def rotate_half(x):
    x1, x2 = x[..., : x.shape[-1] // 2], x[..., x.shape[-1] // 2 :]
    return np.concatenate((-x2, x1), axis=-1)


def setup_inputs():
    s = kspread(HID)
    hidden_states = np.random.standard_normal((B, S, HID)) * s
    hidden_states_words, hidden_states_scales = pack4(hidden_states.reshape(B * S, HID).T)
    cos = bf(np.random.uniform(size=(S, D)))
    sin = bf(np.random.uniform(size=(S, D)))
    words, scales = pack4(np.random.standard_normal((HID, QKV)) * 2.0 / np.sqrt(HID) / s[:, None])
    return {"hidden_states_words": hidden_states_words,
            "hidden_states_scales": hidden_states_scales,
            "cos": cos,
            "sin": sin,
            "w_qkv_words": words,
            "w_qkv_scales": scales}


def reference(hidden_states_words, hidden_states_scales, cos, sin, w_qkv_words, w_qkv_scales):
    qkv = unpack4(hidden_states_words, hidden_states_scales).T.reshape(B, S, HID) @ unpack4(w_qkv_words, w_qkv_scales)
    qkv = qkv.reshape(B, S, 3 * H, D)
    q, k, v = qkv[:, :, :H], qkv[:, :, H:2 * H], qkv[:, :, 2 * H:]
    c = f64(cos)[:, None, :]
    sn = f64(sin)[:, None, :]
    q_rot = q * c + rotate_half(q) * sn
    k_rot = k * c + rotate_half(k) * sn
    return q_rot, k_rot, v

@@ -1,0 +1,234 @@
+from contextlib import ExitStack
+
+import concourse.mybir as mybir
+
+TOKENS, HIDDEN, HEADS, HEAD_DIM = 384, 4096, 8, 128
+QKV = 3 * HEADS * HEAD_DIM
+FLOPS = 2 * TOKENS * HIDDEN * QKV
+
+F32 = mybir.dt.float32
+BF16 = mybir.dt.bfloat16
+U8 = mybir.dt.uint8
+I32 = mybir.dt.int32
+FP4X4 = mybir.dt.float4_e2m1fn_x4
+MULT = mybir.AluOpType.mult
+ADD = mybir.AluOpType.add
+
+P = 128
+PASSES = HIDDEN // 512
+TOKEN_TILES = TOKENS // P
+CHUNK = 512
+HALF = HEAD_DIM // 2
+HEADS_PER_CHUNK = CHUNK // HEAD_DIM
+
+H_CODE_PIECES = ((0, 1), (1, 4), (4, 8))
+H_SCALE_RUNS = ((0, 4), (4, 8))
+Q_CODE_PIECES = ((0, 1), (1, 2), (2, 4), (4, 6), (6, 8))
+Q_SCALE_RUNS = ((0, 2), (2, 5), (5, 8))
+LATE_CODE_PIECES = ((0, 4), (4, 8))
+N_WARM = 8
+
+
+def tile_attention_pa_kernel(tc, h_words, h_scales, cos, sin, w_words, w_scales, out_q, out_k, out_v):
+    nc = tc.nc
+
+    with ExitStack() as ctx:
+        keep = ctx.enter_context(tc.tile_pool(name="keep", bufs=1))
+        tmp = ctx.enter_context(tc.tile_pool(name="tmp", bufs=3))
+        psum = ctx.enter_context(tc.psum_pool(name="psum", bufs=8))
+        ctx.enter_context(tc.manual_schedule())
+
+        def alloc(pieces, width, name):
+            tiles = []
+            for i, (g0, g1) in enumerate(pieces):
+                t = keep.tile([P, g1 - g0, width], U8, name="%s%d" % (name, i), align_bytes=64)
+                tiles.append(t)
+            return tiles
+
+        def by_pass(pieces, tiles):
+            view = {}
+            for (g0, g1), t in zip(pieces, tiles):
+                for g in range(g0, g1):
+                    view[g] = t[:, g - g0, :]
+            return view
+
+        def zero(plane):
+            nc.vector.memset(plane[:].bitcast(I32), 0)
+
+        def load_codes(dst, src, piece, b0, b1):
+            g0, g1 = piece
+            nc.sync.dma_start(
+                out=dst[:].bitcast(I32),
+                in_=src[g0:g1, :, b0:b1].rearrange("g p b -> p g b").bitcast(I32),
+            )
+
+        def load_scales(plane, src, run, c0, c1):
+            g0, g1 = run
+            for quad in range(4):
+                nc.sync.dma_start(
+                    out=plane[32 * quad : 32 * quad + 4, :, :].bitcast(I32),
+                    in_=src[g0:g1, 4 * quad : 4 * quad + 4, c0:c1].rearrange("g r n -> r g n").bitcast(I32),
+                )
+
+        hc_t = alloc(H_CODE_PIECES, 2 * TOKENS, "hc")
+        hs_t = alloc(H_SCALE_RUNS, TOKENS, "hs")
+        qc_t = alloc(Q_CODE_PIECES, 4 * CHUNK, "qc")
+        qs_t = alloc(Q_SCALE_RUNS, 2 * CHUNK, "qs")
+        late_c = {}
+        late_s = {}
+        for n in range(2, 6):
+            late_c[n] = alloc(LATE_CODE_PIECES, 2 * CHUNK, "wc%d_" % n)
+            late_s[n] = alloc(((0, PASSES),), CHUNK, "ws%d_" % n)
+        hc = by_pass(H_CODE_PIECES, hc_t)
+        hs = by_pass(H_SCALE_RUNS, hs_t)
+        qc = by_pass(Q_CODE_PIECES, qc_t)
+        qs = by_pass(Q_SCALE_RUNS, qs_t)
+
+        zeros = keep.tile([P, CHUNK], BF16, name="zeros")
+        cos_sb = keep.tile([P, TOKEN_TILES, HEAD_DIM], BF16, name="cos_sb")
+        sin_sb = keep.tile([P, TOKEN_TILES, HEAD_DIM], BF16, name="sin_sb")
+        nsin_lo = keep.tile([P, TOKEN_TILES, HALF], BF16, name="nsin_lo")
+
+        nc.gpsimd.memset(zeros[:], 0.0)
+        nc.gpsimd.dma_start(out=cos_sb[:], in_=cos.rearrange("(m p) d -> p m d", p=P))
+        nc.gpsimd.dma_start(out=sin_sb[:], in_=sin.rearrange("(m p) d -> p m d", p=P))
+
+        for plane in (hs_t[0], qs_t[0], qs_t[1], hs_t[1], qs_t[2]):
+            zero(plane)
+        for n in range(2, 6):
+            zero(late_s[n][0])
+        nc.vector.tensor_scalar_mul(out=nsin_lo[:], in0=sin_sb[:, :, 0:HALF], scalar1=-1.0)
+
+        load_codes(hc_t[0], h_words, H_CODE_PIECES[0], 0, 2 * TOKENS)
+        load_codes(qc_t[0], w_words, Q_CODE_PIECES[0], 0, 4 * CHUNK)
+        load_scales(hs_t[0], h_scales, H_SCALE_RUNS[0], 0, TOKENS)
+        load_scales(qs_t[0], w_scales, Q_SCALE_RUNS[0], 0, 2 * CHUNK)
+        load_codes(qc_t[1], w_words, Q_CODE_PIECES[1], 0, 4 * CHUNK)
+        load_codes(hc_t[1], h_words, H_CODE_PIECES[1], 0, 2 * TOKENS)
+        load_scales(qs_t[1], w_scales, Q_SCALE_RUNS[1], 0, 2 * CHUNK)
+        load_codes(qc_t[2], w_words, Q_CODE_PIECES[2], 0, 4 * CHUNK)
+        load_codes(hc_t[2], h_words, H_CODE_PIECES[2], 0, 2 * TOKENS)
+        load_scales(hs_t[1], h_scales, H_SCALE_RUNS[1], 0, TOKENS)
+        load_codes(qc_t[3], w_words, Q_CODE_PIECES[3], 0, 4 * CHUNK)
+        load_scales(qs_t[2], w_scales, Q_SCALE_RUNS[2], 0, 2 * CHUNK)
+        load_codes(qc_t[4], w_words, Q_CODE_PIECES[4], 0, 4 * CHUNK)
+
+        def load_late_scales(n):
+            load_scales(late_s[n][0], w_scales, (0, PASSES), n * CHUNK, (n + 1) * CHUNK)
+
+        def load_late_codes(n):
+            for i, piece in enumerate(LATE_CODE_PIECES):
+                load_codes(late_c[n][i], w_words, piece, 2 * n * CHUNK, 2 * (n + 1) * CHUNK)
+
+        load_late_scales(2)
+        load_late_codes(2)
+        load_late_scales(3)
+        load_late_scales(4)
+        load_late_codes(3)
+        load_late_codes(4)
+        load_late_scales(5)
+        load_late_codes(5)
+
+        warm = psum.tile([P, CHUNK], F32, name="warm", tag="acc")
+        for i in range(N_WARM):
+            nc.tensor.matmul(out=warm[:], lhsT=zeros[:, 0:P], rhs=zeros[:], start=True, stop=True)
+
+        def mx_pass(acc, g, m, codes, scales):
+            nc.tensor.matmul_mx(
+                out=acc,
+                lhsT=hc[g][:, 2 * P * m : 2 * P * (m + 1)].bitcast(FP4X4),
+                lhsT_scale=hs[g][:, P * m : P * (m + 1)],
+                rhs=codes.bitcast(FP4X4),
+                rhs_scale=scales,
+                start=(g == 0),
+                stop=(g == PASSES - 1),
+            )
+
+        counter = [0]
+
+        def rope(acc, m, dst):
+            counter[0] += 1
+            res = keep.tile([P, CHUNK], F32, name="res%d" % counter[0])
+            rot = tmp.tile([P, CHUNK], F32, name="rot")
+            x = acc[:].rearrange("p (h t d) -> p h t d", t=2, d=HALF)
+            r = rot[:].rearrange("p (h t d) -> p h t d", t=2, d=HALF)
+            nc.vector.tensor_tensor(
+                out=res[:].rearrange("p (h d) -> p h d", d=HEAD_DIM),
+                in0=acc[:].rearrange("p (h d) -> p h d", d=HEAD_DIM),
+                in1=cos_sb[:, m : m + 1, :].to_broadcast([P, HEADS_PER_CHUNK, HEAD_DIM]),
+                op=MULT,
+            )
+            nc.vector.tensor_tensor(
+                out=r[:, :, 0, :],
+                in0=x[:, :, 1, :],
+                in1=nsin_lo[:, m : m + 1, :].to_broadcast([P, HEADS_PER_CHUNK, HALF]),
+                op=MULT,
+            )
+            nc.vector.tensor_tensor(
+                out=r[:, :, 1, :],
+                in0=x[:, :, 0, :],
+                in1=sin_sb[:, m : m + 1, HALF:HEAD_DIM].to_broadcast([P, HEADS_PER_CHUNK, HALF]),
+                op=MULT,
+            )
+            nc.gpsimd.tensor_tensor(out=res[:], in0=res[:], in1=rot[:], op=ADD)
+            nc.sync.dma_start(out=dst, in_=res[:].rearrange("p (h d) -> p h d", d=HEAD_DIM))
+
+        def copy_out(acc, width, dst):
+            counter[0] += 1
+            res = keep.tile([P, width], F32, name="res%d" % counter[0])
+            nc.scalar.copy(out=res[:], in_=acc[:])
+            nc.scalar.dma_start(out=dst, in_=res[:].rearrange("p (h d) -> p h d", d=HEAD_DIM))
+
+        def out_rows(out, m, col0, width):
+            h0 = col0 // HEAD_DIM
+            return out[0, P * m : P * (m + 1), h0 : h0 + width // HEAD_DIM, :]
+
+        accs = {}
+        for m in range(TOKEN_TILES):
+            for n in range(2):
+                acc = psum.tile([P, CHUNK], F32, name="acc", tag="acc")
+                accs[(m, n)] = acc
+        for g in range(PASSES):
+            for m in range(TOKEN_TILES):
+                for n in range(2):
+                    mx_pass(
+                        accs[(m, n)][:], g, m,
+                        qc[g][:, 2 * CHUNK * n : 2 * CHUNK * (n + 1)],
+                        qs[g][:, CHUNK * n : CHUNK * (n + 1)],
+                    )
+        for m in range(TOKEN_TILES):
+            for n in range(2):
+                rope(accs[(m, n)], m, out_rows(out_q, m, CHUNK * n, CHUNK))
+
+        def late_operand(n, g, c0, c1):
+            piece = g // 4
+            return late_c[n][piece][:, g - 4 * piece, 2 * c0 : 2 * c1], late_s[n][0][:, g, c0:c1]
+
+        accs = {}
+        for m in range(TOKEN_TILES):
+            acc = psum.tile([P, CHUNK], F32, name="acc", tag="acc")
+            accs[m] = acc
+        for g in range(PASSES):
+            for m in range(TOKEN_TILES):
+                codes, scales = late_operand(2, g, 0, CHUNK)
+                mx_pass(accs[m][:], g, m, codes, scales)
+        for m in range(TOKEN_TILES):
+            rope(accs[m], m, out_rows(out_k, m, 0, CHUNK))
+
+        def group(n, m, c0, c1):
+            acc = psum.tile([P, c1 - c0], F32, name="acc", tag="acc")
+            for g in range(PASSES):
+                codes, scales = late_operand(n, g, c0, c1)
+                mx_pass(acc[:], g, m, codes, scales)
+            return acc
+
+        for m in range(TOKEN_TILES):
+            rope(group(3, m, 0, CHUNK), m, out_rows(out_k, m, CHUNK, CHUNK))
+        for n in (4, 5):
+            for m in range(TOKEN_TILES):
+                if (n, m) == (5, TOKEN_TILES - 1):
+                    for c0 in (0, CHUNK // 2):
+                        acc = group(n, m, c0, c0 + CHUNK // 2)
+                        copy_out(acc, CHUNK // 2, out_rows(out_v, m, CHUNK * (n - 4) + c0, CHUNK // 2))
+                else:
+                    copy_out(group(n, m, 0, CHUNK), CHUNK, out_rows(out_v, m, CHUNK * (n - 4), CHUNK))

@@ -64,10 +64,10 @@ def tile_attention_pa_kernel(tc, h_words, h_scales, cos, sin, w_words, w_scales,
 
         def load_scales(plane, src, run, c0, c1):
             g0, g1 = run
-            for quad in range(4):
+            for r in range(4):
                 nc.sync.dma_start(
-                    out=plane[32 * quad : 32 * quad + 4, :, :].bitcast(I32),
-                    in_=src[g0:g1, 4 * quad : 4 * quad + 4, c0:c1].rearrange("g r n -> r g n").bitcast(I32),
+                    out=plane[r : P : 32, :, :].bitcast(I32),
+                    in_=src[g0:g1, r : 16 : 4, c0:c1].rearrange("g q n -> q g n").bitcast(I32),
                 )
 
         hc_t = alloc(H_CODE_PIECES, 2 * TOKENS, "hc")

@@ -21,10 +21,10 @@ CHUNK = 512
 HALF = HEAD_DIM // 2
 HEADS_PER_CHUNK = CHUNK // HEAD_DIM
 
-H_CODE_PIECES = ((0, 1), (1, 4), (4, 8))
+H_CODE_PIECES = ((0, 1), (1, 5), (5, 8))
 H_SCALE_RUNS = ((0, 4), (4, 8))
-Q_CODE_PIECES = ((0, 1), (1, 2), (2, 4), (4, 6), (6, 8))
-Q_SCALE_RUNS = ((0, 2), (2, 5), (5, 8))
+Q_CODE_PIECES = ((0, 1), (1, 2), (2, 3), (3, 4), (4, 6), (6, 8))
+Q_SCALE_RUNS = ((0, 3), (3, 5), (5, 8))
 LATE_CODE_PIECES = ((0, 4), (4, 8))
 N_WARM = 8
 
@@ -62,9 +62,9 @@ def tile_attention_pa_kernel(tc, h_words, h_scales, cos, sin, w_words, w_scales,
                 in_=src[g0:g1, :, b0:b1].rearrange("g p b -> p g b").bitcast(I32),
             )
 
-        def load_scales(plane, src, run, c0, c1):
+        def load_scales(plane, src, run, c0, c1, rows=(0, 1, 2, 3)):
             g0, g1 = run
-            for r in range(4):
+            for r in rows:
                 nc.sync.dma_start(
                     out=plane[r : P : 32, :, :].bitcast(I32),
                     in_=src[g0:g1, r : 16 : 4, c0:c1].rearrange("g q n -> q g n").bitcast(I32),
@@ -93,25 +93,38 @@ def tile_attention_pa_kernel(tc, h_words, h_scales, cos, sin, w_words, w_scales,
         nc.gpsimd.dma_start(out=cos_sb[:], in_=cos.rearrange("(m p) d -> p m d", p=P))
         nc.gpsimd.dma_start(out=sin_sb[:], in_=sin.rearrange("(m p) d -> p m d", p=P))
 
-        for plane in (hs_t[0], qs_t[0], qs_t[1], hs_t[1], qs_t[2]):
+        for plane in (qs_t[0], hs_t[0], qs_t[1], hs_t[1], qs_t[2]):
             zero(plane)
         for n in range(2, 6):
             zero(late_s[n][0])
         nc.vector.tensor_scalar_mul(out=nsin_lo[:], in0=sin_sb[:, :, 0:HALF], scalar1=-1.0)
 
-        load_codes(hc_t[0], h_words, H_CODE_PIECES[0], 0, 2 * TOKENS)
-        load_codes(qc_t[0], w_words, Q_CODE_PIECES[0], 0, 4 * CHUNK)
-        load_scales(hs_t[0], h_scales, H_SCALE_RUNS[0], 0, TOKENS)
-        load_scales(qs_t[0], w_scales, Q_SCALE_RUNS[0], 0, 2 * CHUNK)
-        load_codes(qc_t[1], w_words, Q_CODE_PIECES[1], 0, 4 * CHUNK)
-        load_codes(hc_t[1], h_words, H_CODE_PIECES[1], 0, 2 * TOKENS)
-        load_scales(qs_t[1], w_scales, Q_SCALE_RUNS[1], 0, 2 * CHUNK)
-        load_codes(qc_t[2], w_words, Q_CODE_PIECES[2], 0, 4 * CHUNK)
-        load_codes(hc_t[2], h_words, H_CODE_PIECES[2], 0, 2 * TOKENS)
-        load_scales(hs_t[1], h_scales, H_SCALE_RUNS[1], 0, TOKENS)
-        load_codes(qc_t[3], w_words, Q_CODE_PIECES[3], 0, 4 * CHUNK)
-        load_scales(qs_t[2], w_scales, Q_SCALE_RUNS[2], 0, 2 * CHUNK)
-        load_codes(qc_t[4], w_words, Q_CODE_PIECES[4], 0, 4 * CHUNK)
+        def load_h_codes(i):
+            load_codes(hc_t[i], h_words, H_CODE_PIECES[i], 0, 2 * TOKENS)
+
+        def load_q_codes(i):
+            load_codes(qc_t[i], w_words, Q_CODE_PIECES[i], 0, 4 * CHUNK)
+
+        def load_h_scales(i):
+            load_scales(hs_t[i], h_scales, H_SCALE_RUNS[i], 0, TOKENS)
+
+        def load_q_scales(i, rows=(0, 1, 2, 3)):
+            load_scales(qs_t[i], w_scales, Q_SCALE_RUNS[i], 0, 2 * CHUNK, rows)
+
+        load_h_codes(0)
+        load_q_codes(0)
+        load_q_scales(0)
+        load_h_scales(0)
+        load_h_codes(1)
+        load_q_codes(1)
+        load_q_codes(2)
+        load_q_codes(3)
+        load_q_scales(1)
+        load_q_codes(4)
+        load_h_scales(1)
+        load_h_codes(2)
+        load_q_scales(2)
+        load_q_codes(5)
 
         def load_late_scales(n):
             load_scales(late_s[n][0], w_scales, (0, PASSES), n * CHUNK, (n + 1) * CHUNK)

@@ -27,6 +27,7 @@ Q_CODE_PIECES = ((0, 1), (1, 2), (2, 3), (3, 4), (4, 6), (6, 8))
 Q_SCALE_RUNS = ((0, 3), (3, 5), (5, 8))
 LATE_CODE_PIECES = ((0, 4), (4, 8))
 N_WARM = 8
+LAST_TILE_CUTS = ((0, 256), (256, 384), (384, 512))
 
 
 def tile_attention_pa_kernel(tc, h_words, h_scales, cos, sin, w_words, w_scales, out_q, out_k, out_v):
@@ -240,8 +241,8 @@ def tile_attention_pa_kernel(tc, h_words, h_scales, cos, sin, w_words, w_scales,
         for n in (4, 5):
             for m in range(TOKEN_TILES):
                 if (n, m) == (5, TOKEN_TILES - 1):
-                    for c0 in (0, CHUNK // 2):
-                        acc = group(n, m, c0, c0 + CHUNK // 2)
-                        copy_out(acc, CHUNK // 2, out_rows(out_v, m, CHUNK * (n - 4) + c0, CHUNK // 2))
+                    for c0, c1 in LAST_TILE_CUTS:
+                        acc = group(n, m, c0, c1)
+                        copy_out(acc, c1 - c0, out_rows(out_v, m, CHUNK * (n - 4) + c0, c1 - c0))
                 else:
                     copy_out(group(n, m, 0, CHUNK), CHUNK, out_rows(out_v, m, CHUNK * (n - 4), CHUNK))

@@ -27,7 +27,6 @@ Q_CODE_PIECES = ((0, 1), (1, 2), (2, 3), (3, 4), (4, 6), (6, 8))
 Q_SCALE_RUNS = ((0, 3), (3, 5), (5, 8))
 LATE_CODE_PIECES = ((0, 4), (4, 8))
 N_WARM = 8
-LAST_TILE_CUTS = ((0, 256), (256, 384), (384, 512))
 
 
 def tile_attention_pa_kernel(tc, h_words, h_scales, cos, sin, w_words, w_scales, out_q, out_k, out_v):
@@ -241,8 +240,16 @@ def tile_attention_pa_kernel(tc, h_words, h_scales, cos, sin, w_words, w_scales,
         for n in (4, 5):
             for m in range(TOKEN_TILES):
                 if (n, m) == (5, TOKEN_TILES - 1):
-                    for c0, c1 in LAST_TILE_CUTS:
-                        acc = group(n, m, c0, c1)
-                        copy_out(acc, c1 - c0, out_rows(out_v, m, CHUNK * (n - 4) + c0, c1 - c0))
+                    front = keep.tile([P, 384], F32, name="front")
+                    acc = group(n, m, 0, 256)
+                    nc.scalar.copy(out=front[:, 0:256], in_=acc[:])
+                    acc = group(n, m, 256, 384)
+                    nc.vector.tensor_copy(out=front[:, 256:384], in_=acc[:])
+                    nc.sync.dma_start(
+                        out=out_rows(out_v, m, CHUNK * (n - 4), 384),
+                        in_=front[:].rearrange("p (h d) -> p h d", d=HEAD_DIM),
+                    )
+                    acc = group(n, m, 384, 512)
+                    copy_out(acc, 128, out_rows(out_v, m, CHUNK * (n - 4) + 384, 128))
                 else:
                     copy_out(group(n, m, 0, CHUNK), CHUNK, out_rows(out_v, m, CHUNK * (n - 4), CHUNK))

@@ -41,7 +41,7 @@ def tile_attention_pa_kernel(tc, h_words, h_scales, cos, sin, w_words, w_scales,
         def alloc(pieces, width, name):
             tiles = []
             for i, (g0, g1) in enumerate(pieces):
-                t = keep.tile([P, g1 - g0, width], U8, name="%s%d" % (name, i), align_bytes=64)
+                t = keep.tile([P, g1 - g0, width], U8, name="%s%d" % (name, i), align_bytes=256)
                 tiles.append(t)
             return tiles
 
@@ -84,9 +84,9 @@ def tile_attention_pa_kernel(tc, h_words, h_scales, cos, sin, w_words, w_scales,
         qc = by_pass(Q_CODE_PIECES, qc_t)
         qs = by_pass(Q_SCALE_RUNS, qs_t)
 
-        zeros = keep.tile([P, CHUNK], BF16, name="zeros")
-        cos_sb = keep.tile([P, TOKEN_TILES, HEAD_DIM], BF16, name="cos_sb")
-        sin_sb = keep.tile([P, TOKEN_TILES, HEAD_DIM], BF16, name="sin_sb")
+        zeros = keep.tile([P, CHUNK], BF16, name="zeros", align_bytes=256)
+        cos_sb = keep.tile([P, TOKEN_TILES, HEAD_DIM], BF16, name="cos_sb", align_bytes=256)
+        sin_sb = keep.tile([P, TOKEN_TILES, HEAD_DIM], BF16, name="sin_sb", align_bytes=256)
         nsin_lo = keep.tile([P, TOKEN_TILES, HALF], BF16, name="nsin_lo")
 
         nc.gpsimd.memset(zeros[:], 0.0)
@@ -161,7 +161,7 @@ def tile_attention_pa_kernel(tc, h_words, h_scales, cos, sin, w_words, w_scales,
 
         def rope(acc, m, dst):
             counter[0] += 1
-            res = keep.tile([P, CHUNK], F32, name="res%d" % counter[0])
+            res = keep.tile([P, CHUNK], F32, name="res%d" % counter[0], align_bytes=256)
             rot = tmp.tile([P, CHUNK], F32, name="rot")
             x = acc[:].rearrange("p (h t d) -> p h t d", t=2, d=HALF)
             r = rot[:].rearrange("p (h t d) -> p h t d", t=2, d=HALF)
@@ -188,7 +188,7 @@ def tile_attention_pa_kernel(tc, h_words, h_scales, cos, sin, w_words, w_scales,
 
         def copy_out(acc, width, dst):
             counter[0] += 1
-            res = keep.tile([P, width], F32, name="res%d" % counter[0])
+            res = keep.tile([P, width], F32, name="res%d" % counter[0], align_bytes=256)
             nc.scalar.copy(out=res[:], in_=acc[:])
             nc.scalar.dma_start(out=dst, in_=res[:].rearrange("p (h d) -> p h d", d=HEAD_DIM))
 
@@ -240,7 +240,7 @@ def tile_attention_pa_kernel(tc, h_words, h_scales, cos, sin, w_words, w_scales,
         for n in (4, 5):
             for m in range(TOKEN_TILES):
                 if (n, m) == (5, TOKEN_TILES - 1):
-                    front = keep.tile([P, 384], F32, name="front")
+                    front = keep.tile([P, 384], F32, name="front", align_bytes=256)
                     acc = group(n, m, 0, 256)
                     nc.scalar.copy(out=front[:, 0:256], in_=acc[:])
                     acc = group(n, m, 256, 384)

@@ -159,18 +159,29 @@ def tile_attention_pa_kernel(tc, h_words, h_scales, cos, sin, w_words, w_scales,
 
         counter = [0]
 
+        pending = []
+
+        def finish_rope():
+            for res, rot, dst in pending:
+                nc.vector.tensor_tensor(out=res[:], in0=res[:], in1=rot[:], op=ADD)
+                nc.sync.dma_start(out=dst, in_=res[:].rearrange("p (h d) -> p h d", d=HEAD_DIM))
+            pending.clear()
+
         def rope(acc, m, dst):
             counter[0] += 1
+            xs = keep.tile([P, CHUNK], F32, name="xs%d" % counter[0])
             res = keep.tile([P, CHUNK], F32, name="res%d" % counter[0], align_bytes=256)
             rot = tmp.tile([P, CHUNK], F32, name="rot")
-            x = acc[:].rearrange("p (h t d) -> p h t d", t=2, d=HALF)
+            nc.scalar.copy(out=xs[:], in_=acc[:])
+            x = xs[:].rearrange("p (h t d) -> p h t d", t=2, d=HALF)
             r = rot[:].rearrange("p (h t d) -> p h t d", t=2, d=HALF)
             nc.vector.tensor_tensor(
                 out=res[:].rearrange("p (h d) -> p h d", d=HEAD_DIM),
-                in0=acc[:].rearrange("p (h d) -> p h d", d=HEAD_DIM),
+                in0=xs[:].rearrange("p (h d) -> p h d", d=HEAD_DIM),
                 in1=cos_sb[:, m : m + 1, :].to_broadcast([P, HEADS_PER_CHUNK, HEAD_DIM]),
                 op=MULT,
             )
+            finish_rope()
             nc.vector.tensor_tensor(
                 out=r[:, :, 0, :],
                 in0=x[:, :, 1, :],
@@ -183,8 +194,7 @@ def tile_attention_pa_kernel(tc, h_words, h_scales, cos, sin, w_words, w_scales,
                 in1=sin_sb[:, m : m + 1, HALF:HEAD_DIM].to_broadcast([P, HEADS_PER_CHUNK, HALF]),
                 op=MULT,
             )
-            nc.gpsimd.tensor_tensor(out=res[:], in0=res[:], in1=rot[:], op=ADD)
-            nc.sync.dma_start(out=dst, in_=res[:].rearrange("p (h d) -> p h d", d=HEAD_DIM))
+            pending.append((res, rot, dst))
 
         def copy_out(acc, width, dst):
             counter[0] += 1
@@ -237,6 +247,7 @@ def tile_attention_pa_kernel(tc, h_words, h_scales, cos, sin, w_words, w_scales,
 
         for m in range(TOKEN_TILES):
             rope(group(3, m, 0, CHUNK), m, out_rows(out_k, m, CHUNK, CHUNK))
+        finish_rope()
         for n in (4, 5):
             for m in range(TOKEN_TILES):
                 if (n, m) == (5, TOKEN_TILES - 1):

from contextlib import ExitStack

import concourse.mybir as mybir

TOKENS, HIDDEN, HEADS, HEAD_DIM = 384, 4096, 8, 128
QKV = 3 * HEADS * HEAD_DIM
FLOPS = 2 * TOKENS * HIDDEN * QKV

F32 = mybir.dt.float32
BF16 = mybir.dt.bfloat16
U8 = mybir.dt.uint8
I32 = mybir.dt.int32
FP4X4 = mybir.dt.float4_e2m1fn_x4
MULT = mybir.AluOpType.mult
ADD = mybir.AluOpType.add

P = 128
PASSES = HIDDEN // 512
TOKEN_TILES = TOKENS // P
CHUNK = 512
HALF = HEAD_DIM // 2
HEADS_PER_CHUNK = CHUNK // HEAD_DIM

H_CODE_PIECES = ((0, 1), (1, 5), (5, 8))
H_SCALE_RUNS = ((0, 4), (4, 8))
Q_CODE_PIECES = ((0, 1), (1, 2), (2, 3), (3, 4), (4, 6), (6, 8))
Q_SCALE_RUNS = ((0, 3), (3, 5), (5, 8))
LATE_CODE_PIECES = ((0, 4), (4, 8))
N_WARM = 8


def tile_attention_pa_kernel(tc, h_words, h_scales, cos, sin, w_words, w_scales, out_q, out_k, out_v):
    nc = tc.nc

    with ExitStack() as ctx:
        keep = ctx.enter_context(tc.tile_pool(name="keep", bufs=1))
        tmp = ctx.enter_context(tc.tile_pool(name="tmp", bufs=3))
        psum = ctx.enter_context(tc.psum_pool(name="psum", bufs=8))
        ctx.enter_context(tc.manual_schedule())

        def alloc(pieces, width, name):
            tiles = []
            for i, (g0, g1) in enumerate(pieces):
                t = keep.tile([P, g1 - g0, width], U8, name="%s%d" % (name, i), align_bytes=256)
                tiles.append(t)
            return tiles

        def by_pass(pieces, tiles):
            view = {}
            for (g0, g1), t in zip(pieces, tiles):
                for g in range(g0, g1):
                    view[g] = t[:, g - g0, :]
            return view

        def zero(plane):
            nc.vector.memset(plane[:].bitcast(I32), 0)

        def load_codes(dst, src, piece, b0, b1):
            g0, g1 = piece
            nc.sync.dma_start(
                out=dst[:].bitcast(I32),
                in_=src[g0:g1, :, b0:b1].rearrange("g p b -> p g b").bitcast(I32),
            )

        def load_scales(plane, src, run, c0, c1, rows=(0, 1, 2, 3)):
            g0, g1 = run
            for r in rows:
                nc.sync.dma_start(
                    out=plane[r : P : 32, :, :].bitcast(I32),
                    in_=src[g0:g1, r : 16 : 4, c0:c1].rearrange("g q n -> q g n").bitcast(I32),
                )

        hc_t = alloc(H_CODE_PIECES, 2 * TOKENS, "hc")
        hs_t = alloc(H_SCALE_RUNS, TOKENS, "hs")
        qc_t = alloc(Q_CODE_PIECES, 4 * CHUNK, "qc")
        qs_t = alloc(Q_SCALE_RUNS, 2 * CHUNK, "qs")
        late_c = {}
        late_s = {}
        for n in range(2, 6):
            late_c[n] = alloc(LATE_CODE_PIECES, 2 * CHUNK, "wc%d_" % n)
            late_s[n] = alloc(((0, PASSES),), CHUNK, "ws%d_" % n)
        hc = by_pass(H_CODE_PIECES, hc_t)
        hs = by_pass(H_SCALE_RUNS, hs_t)
        qc = by_pass(Q_CODE_PIECES, qc_t)
        qs = by_pass(Q_SCALE_RUNS, qs_t)

        zeros = keep.tile([P, CHUNK], BF16, name="zeros", align_bytes=256)
        cos_sb = keep.tile([P, TOKEN_TILES, HEAD_DIM], BF16, name="cos_sb", align_bytes=256)
        sin_sb = keep.tile([P, TOKEN_TILES, HEAD_DIM], BF16, name="sin_sb", align_bytes=256)
        nsin_lo = keep.tile([P, TOKEN_TILES, HALF], BF16, name="nsin_lo")

        nc.gpsimd.memset(zeros[:], 0.0)
        nc.gpsimd.dma_start(out=cos_sb[:], in_=cos.rearrange("(m p) d -> p m d", p=P))
        nc.gpsimd.dma_start(out=sin_sb[:], in_=sin.rearrange("(m p) d -> p m d", p=P))

        for plane in (qs_t[0], hs_t[0], qs_t[1], hs_t[1], qs_t[2]):
            zero(plane)
        for n in range(2, 6):
            zero(late_s[n][0])
        nc.vector.tensor_scalar_mul(out=nsin_lo[:], in0=sin_sb[:, :, 0:HALF], scalar1=-1.0)

        def load_h_codes(i):
            load_codes(hc_t[i], h_words, H_CODE_PIECES[i], 0, 2 * TOKENS)

        def load_q_codes(i):
            load_codes(qc_t[i], w_words, Q_CODE_PIECES[i], 0, 4 * CHUNK)

        def load_h_scales(i):
            load_scales(hs_t[i], h_scales, H_SCALE_RUNS[i], 0, TOKENS)

        def load_q_scales(i, rows=(0, 1, 2, 3)):
            load_scales(qs_t[i], w_scales, Q_SCALE_RUNS[i], 0, 2 * CHUNK, rows)

        load_h_codes(0)
        load_q_codes(0)
        load_q_scales(0)
        load_h_scales(0)
        load_h_codes(1)
        load_q_codes(1)
        load_q_codes(2)
        load_q_codes(3)
        load_q_scales(1)
        load_q_codes(4)
        load_h_scales(1)
        load_h_codes(2)
        load_q_scales(2)
        load_q_codes(5)

        def load_late_scales(n):
            load_scales(late_s[n][0], w_scales, (0, PASSES), n * CHUNK, (n + 1) * CHUNK)

        def load_late_codes(n):
            for i, piece in enumerate(LATE_CODE_PIECES):
                load_codes(late_c[n][i], w_words, piece, 2 * n * CHUNK, 2 * (n + 1) * CHUNK)

        load_late_scales(2)
        load_late_codes(2)
        load_late_scales(3)
        load_late_scales(4)
        load_late_codes(3)
        load_late_codes(4)
        load_late_scales(5)
        load_late_codes(5)

        warm = psum.tile([P, CHUNK], F32, name="warm", tag="acc")
        for i in range(N_WARM):
            nc.tensor.matmul(out=warm[:], lhsT=zeros[:, 0:P], rhs=zeros[:], start=True, stop=True)

        def mx_pass(acc, g, m, codes, scales):
            nc.tensor.matmul_mx(
                out=acc,
                lhsT=hc[g][:, 2 * P * m : 2 * P * (m + 1)].bitcast(FP4X4),
                lhsT_scale=hs[g][:, P * m : P * (m + 1)],
                rhs=codes.bitcast(FP4X4),
                rhs_scale=scales,
                start=(g == 0),
                stop=(g == PASSES - 1),
            )

        counter = [0]

        pending = []

        def finish_rope():
            for res, rot, dst in pending:
                nc.vector.tensor_tensor(out=res[:], in0=res[:], in1=rot[:], op=ADD)
                nc.sync.dma_start(out=dst, in_=res[:].rearrange("p (h d) -> p h d", d=HEAD_DIM))
            pending.clear()

        def rope(acc, m, dst):
            counter[0] += 1
            xs = keep.tile([P, CHUNK], F32, name="xs%d" % counter[0])
            res = keep.tile([P, CHUNK], F32, name="res%d" % counter[0], align_bytes=256)
            rot = tmp.tile([P, CHUNK], F32, name="rot")
            nc.scalar.copy(out=xs[:], in_=acc[:])
            x = xs[:].rearrange("p (h t d) -> p h t d", t=2, d=HALF)
            r = rot[:].rearrange("p (h t d) -> p h t d", t=2, d=HALF)
            nc.vector.tensor_tensor(
                out=res[:].rearrange("p (h d) -> p h d", d=HEAD_DIM),
                in0=xs[:].rearrange("p (h d) -> p h d", d=HEAD_DIM),
                in1=cos_sb[:, m : m + 1, :].to_broadcast([P, HEADS_PER_CHUNK, HEAD_DIM]),
                op=MULT,
            )
            finish_rope()
            nc.vector.tensor_tensor(
                out=r[:, :, 0, :],
                in0=x[:, :, 1, :],
                in1=nsin_lo[:, m : m + 1, :].to_broadcast([P, HEADS_PER_CHUNK, HALF]),
                op=MULT,
            )
            nc.vector.tensor_tensor(
                out=r[:, :, 1, :],
                in0=x[:, :, 0, :],
                in1=sin_sb[:, m : m + 1, HALF:HEAD_DIM].to_broadcast([P, HEADS_PER_CHUNK, HALF]),
                op=MULT,
            )
            pending.append((res, rot, dst))

        def copy_out(acc, width, dst):
            counter[0] += 1
            res = keep.tile([P, width], F32, name="res%d" % counter[0], align_bytes=256)
            nc.scalar.copy(out=res[:], in_=acc[:])
            nc.scalar.dma_start(out=dst, in_=res[:].rearrange("p (h d) -> p h d", d=HEAD_DIM))

        def out_rows(out, m, col0, width):
            h0 = col0 // HEAD_DIM
            return out[0, P * m : P * (m + 1), h0 : h0 + width // HEAD_DIM, :]

        accs = {}
        for m in range(TOKEN_TILES):
            for n in range(2):
                acc = psum.tile([P, CHUNK], F32, name="acc", tag="acc")
                accs[(m, n)] = acc
        for g in range(PASSES):
            for m in range(TOKEN_TILES):
                for n in range(2):
                    mx_pass(
                        accs[(m, n)][:], g, m,
                        qc[g][:, 2 * CHUNK * n : 2 * CHUNK * (n + 1)],
                        qs[g][:, CHUNK * n : CHUNK * (n + 1)],
                    )
        for m in range(TOKEN_TILES):
            for n in range(2):
                rope(accs[(m, n)], m, out_rows(out_q, m, CHUNK * n, CHUNK))

        def late_operand(n, g, c0, c1):
            piece = g // 4
            return late_c[n][piece][:, g - 4 * piece, 2 * c0 : 2 * c1], late_s[n][0][:, g, c0:c1]

        accs = {}
        for m in range(TOKEN_TILES):
            acc = psum.tile([P, CHUNK], F32, name="acc", tag="acc")
            accs[m] = acc
        for g in range(PASSES):
            for m in range(TOKEN_TILES):
                codes, scales = late_operand(2, g, 0, CHUNK)
                mx_pass(accs[m][:], g, m, codes, scales)
        for m in range(TOKEN_TILES):
            rope(accs[m], m, out_rows(out_k, m, 0, CHUNK))

        def group(n, m, c0, c1):
            acc = psum.tile([P, c1 - c0], F32, name="acc", tag="acc")
            for g in range(PASSES):
                codes, scales = late_operand(n, g, c0, c1)
                mx_pass(acc[:], g, m, codes, scales)
            return acc

        for m in range(TOKEN_TILES):
            rope(group(3, m, 0, CHUNK), m, out_rows(out_k, m, CHUNK, CHUNK))
        finish_rope()
        for n in (4, 5):
            for m in range(TOKEN_TILES):
                if (n, m) == (5, TOKEN_TILES - 1):
                    front = keep.tile([P, 384], F32, name="front", align_bytes=256)
                    acc = group(n, m, 0, 256)
                    nc.scalar.copy(out=front[:, 0:256], in_=acc[:])
                    acc = group(n, m, 256, 384)
                    nc.vector.tensor_copy(out=front[:, 256:384], in_=acc[:])
                    nc.sync.dma_start(
                        out=out_rows(out_v, m, CHUNK * (n - 4), 384),
                        in_=front[:].rearrange("p (h d) -> p h d", d=HEAD_DIM),
                    )
                    acc = group(n, m, 384, 512)
                    copy_out(acc, 128, out_rows(out_v, m, CHUNK * (n - 4) + 384, 128))
                else:
                    copy_out(group(n, m, 0, CHUNK), CHUNK, out_rows(out_v, m, CHUNK * (n - 4), CHUNK))
